import numpy as np
import ml_dtypes


def mxq(x, axis, fmt="e4m3"):
    dtype, down = {"e4m3": (ml_dtypes.float8_e4m3fn, 7), "e5m2": (ml_dtypes.float8_e5m2, 14)}[fmt]
    v = np.moveaxis(np.asarray(x, np.float32).astype(ml_dtypes.bfloat16).astype(np.float64), axis, -1)
    blocks = v.reshape(v.shape[:-1] + (-1, 32))
    amax = np.abs(blocks).max(-1, keepdims=True)
    byte = np.maximum(np.where(amax > 0, np.frexp(amax)[1] - 1 + 127, 0) - down, 1)
    scale = np.exp2(byte - 127.0)
    codes = (blocks / scale).astype(np.float32).astype(dtype).astype(np.float64)
    return np.moveaxis((codes * scale).reshape(v.shape), -1, axis)


WIDE = False


def mx_kscale(k):
    if not WIDE:
        return np.ones(k)
    levels = np.array([10, -10, 5, -5, 0])
    if k % 512:
        return np.exp2(np.random.permutation(np.resize(levels, k // 32))).repeat(32)
    a = np.empty((k // 512, 16))
    for p in range(k // 512):
        a[p, :8] = np.random.permutation(np.resize(levels, 8))
        for g in range(8):
            far = levels[np.abs(levels - a[p, g]) >= 10]
            a[p, g + 8] = far[np.random.randint(len(far))]
    return np.exp2(a.ravel()).repeat(32)


BF16 = ml_dtypes.bfloat16


def bf(x):
    return np.asarray(x, np.float32).astype(BF16)


def f64(x):
    return np.asarray(x).astype(np.float64)


B, T, C, HS, DW, DA, DV, DG = 4, 128, 512, 64, 128, 128, 128, 256


def sigmoid(z):
    return 1.0 / (1.0 + np.exp(-z))


def setup_inputs():
    s = mx_kscale(C)
    return {
        "x": bf(np.random.standard_normal((B, T, C)) * s),
        "v_first": bf(np.random.standard_normal((B, T, C))),
        "x_v": bf(np.random.uniform(0.0, 1.0, C)),
        "Wv": bf(np.random.standard_normal((C, C)) / np.sqrt(C) / s[None, :]),
        "v0": bf(np.random.standard_normal(C)),
        "xv_v1": bf(0.8 * np.random.standard_normal((B, T, DV))),
        "v2": bf(np.random.standard_normal((DV, C)) / np.sqrt(DV)),
    }


def reference(x, v_first, x_v, Wv, v0, xv_v1, v2):
    x = f64(x)
    xprev = np.concatenate([np.zeros_like(x[:, :1]), x[:, :-1]], axis=1)
    xx = xprev - x
    xv = x + xx * f64(x_v)
    v = mxq(xv, 2, "e4m3") @ mxq(f64(Wv), 1, "e4m3").T
    v = v + (f64(v_first) - v) * sigmoid(f64(v0) + f64(xv_v1) @ f64(v2))
    return v

@@ -1,0 +1,212 @@
+from contextlib import ExitStack
+
+import concourse.mybir as mybir
+from concourse.masks import make_identity
+
+BF16 = mybir.dt.bfloat16
+F32 = mybir.dt.float32
+U32 = mybir.dt.uint32
+U8 = mybir.dt.uint8
+FP8X4 = mybir.dt.float8_e4m3fn_x4
+ALU = mybir.AluOpType
+ACT = mybir.ActivationFunctionType
+
+P = 128
+B, T, C, DV = 4, 128, 512, 128
+PACK = 4
+HALVES = 2
+ROWS = 256
+WORDS = C // 2
+
+FLOPS = 2 * B * T * C * C + 2 * B * T * DV * C
+
+
+def tile_full_tmix_params_pb_s_kernel(tc, x, v_first, x_v, Wv, v0, xv_v1, v2, out):
+    nc = tc.nc
+    with ExitStack() as ctx:
+        keep = ctx.enter_context(tc.tile_pool(name="keep", bufs=1))
+        banks = ctx.enter_context(tc.psum_pool(name="banks", bufs=8))
+        ctx.enter_context(tc.manual_schedule())
+
+        mix_bf = keep.tile([P, PACK], BF16)
+        nc.scalar.dma_start(out=mix_bf[:], in_=x_v.rearrange("(p j) -> p j", j=PACK))
+        v0_col = keep.tile([P, C // P], BF16)
+        with nc.allow_non_contiguous_dma(reason="512 single elements, once"):
+            nc.scalar.dma_start(out=v0_col[:], in_=v0.rearrange("(m p) -> p m", p=P))
+        a_sb = keep.tile([P, B * DV], BF16)
+        nc.sync.dma_start(out=a_sb[:].rearrange("t (b k) -> t b k", b=B), in_=xv_v1.rearrange("b t k -> t b k"))
+        x_sb = keep.tile([P, B * C], BF16)
+        for h in range(HALVES):
+            nc.sync.dma_start(
+                out=x_sb[:, 2 * h * C : (2 * h + 2) * C].rearrange("t (b c) -> t b c", b=2),
+                in_=x[2 * h : 2 * h + 2].rearrange("b t c -> t b c"),
+            )
+        v2_sb = keep.tile([P, C], BF16)
+        nc.sync.dma_start(out=v2_sb[:], in_=v2)
+        w_sb = keep.tile([P, 4 * C], BF16)
+        for h in range(HALVES):
+            nc.sync.dma_start(
+                out=w_sb[:, 2 * h * C : (2 * h + 2) * C].rearrange("o (m k) -> o m k", m=2),
+                in_=Wv[h * ROWS : (h + 1) * ROWS, :].rearrange("(m o) k -> o m k", o=P),
+            )
+        vf_sb = keep.tile([P, B, C], BF16)
+        nc.sync.dma_start(out=vf_sb[:], in_=v_first.rearrange("b t c -> t b c"))
+
+        warm = keep.tile([P, 1], F32)
+        nc.vector.memset(warm[:], 0.0)
+        nc.scalar.activation(out=warm[:], in_=warm[:], func=ACT.Sigmoid)
+
+        ident_bf = keep.tile([P, P], BF16)
+        make_identity(nc, ident_bf[:])
+        ident_f32 = keep.tile([P, P], F32)
+        make_identity(nc, ident_f32[:])
+
+        mix = keep.tile([P, PACK], F32)
+        nc.vector.tensor_copy(out=mix[:], in_=mix_bf[:])
+        stay = keep.tile([P, PACK], F32)
+        nc.vector.tensor_scalar(out=stay[:], in0=mix[:], scalar1=-1.0, scalar2=1.0, op0=ALU.mult, op1=ALU.add)
+        v0_rep = keep.tile([P, C // P, P], F32)
+        nc.vector.tensor_copy(out=v0_rep[:], in_=v0_col[:].unsqueeze(2).to_broadcast([P, C // P, P]))
+
+        aT = keep.tile([P, B * T], BF16)
+        gate = keep.tile([P, B, C], F32)
+        from_first = keep.tile([P, B, C], F32)
+        x_words = x_sb[:].bitcast(F32)
+        kept = keep.tile([P, HALVES, PACK, ROWS], F32)
+        xv_slot = keep.tile([P, HALVES, PACK, ROWS], BF16)
+        xv_grp = keep.tile([P, HALVES, ROWS, PACK], BF16, align_bytes=64)
+        x_codes = keep.tile([P, B * T], U32, align_bytes=64)
+        x_scales = keep.tile([P, B * T], U8, align_bytes=64)
+        w_words = w_sb[:].bitcast(F32)
+        w_grp = keep.tile([P, C * PACK], BF16, align_bytes=64)
+        w_grp_words = w_grp[:].bitcast(F32).rearrange("p (o u) -> p o u", u=2)
+        w_codes = keep.tile([P, C], U32, align_bytes=64)
+        w_scales = keep.tile([P, C], U8, align_bytes=64)
+        minus_p = keep.tile([P, B, C], F32)
+        res = keep.tile([P, B, C], F32)
+
+        def by_sequence(plane):
+            return plane.rearrange("p (l t) -> p l t", l=2)
+
+        def transpose_x(h, u):
+            bank = banks.tile([P, ROWS], F32, tag="bank", name="x_bank")
+            for l in range(2):
+                row = (2 * h + l) * WORDS
+                nc.tensor.transpose(bank[:, l * T : (l + 1) * T], x_words[:, row + u : row + WORDS : 2], ident_f32[:])
+            return bank[:].bitcast(BF16).rearrange("p (l t e) -> p l t e", l=2, e=2)
+
+        def keep_part(h, u, xT):
+            for e in range(2):
+                j = 2 * u + e
+                nc.scalar.activation(
+                    out=by_sequence(kept[:, h, j, :]), in_=xT[:, :, :, e], func=ACT.Copy, scale=stay[:, j : j + 1]
+                )
+
+        def add_previous(h, u, xT):
+            for e in range(2):
+                j = 2 * u + e
+                nc.vector.scalar_tensor_tensor(
+                    out=by_sequence(xv_slot[:, h, j, :])[:, :, 1:T],
+                    in0=xT[:, :, 0 : T - 1, e],
+                    scalar=mix[:, j : j + 1],
+                    in1=by_sequence(kept[:, h, j, :])[:, :, 1:T],
+                    op0=ALU.mult,
+                    op1=ALU.add,
+                )
+
+        def first_tokens(h):
+            nc.vector.tensor_copy(
+                out=xv_slot[:, h].rearrange("p j (l t) -> p j l t", l=2)[:, :, :, 0],
+                in_=kept[:, h].rearrange("p j (l t) -> p j l t", l=2)[:, :, :, 0],
+            )
+
+        def regroup(h):
+            nc.vector.tensor_copy(
+                out=xv_grp[:, h].rearrange("p (c i) j -> p c j i", i=4),
+                in_=xv_slot[:, h].rearrange("p j (c i) -> p c j i", i=4),
+            )
+
+        def quantise_x(h):
+            cols = slice(h * ROWS, (h + 1) * ROWS)
+            nc.vector.quantize_mx(
+                out=x_codes[:, cols].bitcast(FP8X4),
+                scales=x_scales[:, cols],
+                in_=xv_grp[:, h].rearrange("p r j -> p (r j)"),
+            )
+
+        def weights(h):
+            bank = banks.tile([P, 2 * ROWS], F32, tag="bank", name="w_bank")
+            view = bank[:].rearrange("p (u l o) -> p u l o", u=2, l=2)
+            for l in range(2):
+                for u in range(2):
+                    row = (2 * h + l) * WORDS
+                    nc.tensor.transpose(view[:, u, l, :], w_words[:, row + u : row + WORDS : 2], ident_f32[:])
+            nc.scalar.copy(
+                out=w_grp_words[:, h * ROWS : (h + 1) * ROWS, :],
+                in_=bank[:].rearrange("p (u o) -> p o u", u=2),
+            )
+
+        def gate_of(b):
+            z = banks.tile([P, C], F32, tag="bank", name="z")
+            for m in range(C // P):
+                nc.tensor.matmul(
+                    out=z[:, m * P : (m + 1) * P],
+                    lhsT=v0_rep[:, m, :],
+                    rhs=ident_f32[:],
+                    is_transpose=True,
+                    start=(m == 0),
+                    stop=False,
+                )
+            nc.tensor.matmul(out=z[:], lhsT=aT[:, b * T : (b + 1) * T], rhs=v2_sb[:], start=False, stop=True)
+            nc.scalar.activation(out=gate[:, b, :], in_=z[:], func=ACT.Sigmoid)
+            nc.gpsimd.tensor_tensor(out=from_first[:, b, :], in0=vf_sb[:, b, :], in1=gate[:, b, :], op=ALU.mult)
+
+        aT_ps = banks.tile([P, B * T], BF16, tag="bank")
+        for b in range(B):
+            nc.tensor.transpose(aT_ps[:, b * T : (b + 1) * T], a_sb[:, b * DV : (b + 1) * DV], ident_bf[:])
+        nc.vector.tensor_copy(out=aT[:], in_=aT_ps[:])
+
+        pieces = [(h, u) for h in range(HALVES) for u in range(2)]
+        xT = {}
+        for h, u in pieces:
+            xT[(h, u)] = transpose_x(h, u)
+        for h, u in pieces:
+            keep_part(h, u, xT[(h, u)])
+        gate_of(0)
+        gate_of(1)
+        weights(0)
+        weights(1)
+        gate_of(2)
+        gate_of(3)
+
+        add_previous(0, 0, xT[(0, 0)])
+        add_previous(0, 1, xT[(0, 1)])
+        first_tokens(0)
+        regroup(0)
+        add_previous(1, 0, xT[(1, 0)])
+        add_previous(1, 1, xT[(1, 1)])
+        quantise_x(0)
+        first_tokens(1)
+        regroup(1)
+        nc.vector.quantize_mx(out=w_codes[:].bitcast(FP8X4), scales=w_scales[:], in_=w_grp[:])
+        quantise_x(1)
+
+        for b in range(B):
+            toks = slice(b * T, (b + 1) * T)
+            p_ps = banks.tile([P, C], F32, tag="bank")
+            nc.tensor.matmul_mx(
+                out=p_ps[:],
+                lhsT=x_codes[:, toks].bitcast(FP8X4),
+                lhsT_scale=x_scales[:, toks],
+                rhs=w_codes[:].bitcast(FP8X4),
+                rhs_scale=w_scales[:],
+                start=True,
+                stop=True,
+            )
+            nc.vector.scalar_tensor_tensor(
+                out=minus_p[:, b, :], in0=gate[:, b, :], scalar=1.0, in1=p_ps[:], op0=ALU.subtract, op1=ALU.mult
+            )
+            engine = nc.gpsimd if b < B // 2 else nc.vector
+            engine.tensor_tensor(out=res[:, b, :], in0=from_first[:, b, :], in1=minus_p[:, b, :], op=ALU.subtract)
+            queue = nc.scalar if b < B // 2 else nc.sync
+            queue.dma_start(out=out[b], in_=res[:, b, :])

@@ -30,17 +30,17 @@ def tile_full_tmix_params_pb_s_kernel(tc, x, v_first, x_v, Wv, v0, xv_v1, v2, ou
 
         mix_bf = keep.tile([P, PACK], BF16)
         nc.scalar.dma_start(out=mix_bf[:], in_=x_v.rearrange("(p j) -> p j", j=PACK))
-        v0_col = keep.tile([P, C // P], BF16)
-        with nc.allow_non_contiguous_dma(reason="512 single elements, once"):
-            nc.scalar.dma_start(out=v0_col[:], in_=v0.rearrange("(m p) -> p m", p=P))
+        v0_bf = keep.tile([P, PACK], BF16)
+        nc.scalar.dma_start(out=v0_bf[:], in_=v0.rearrange("(p j) -> p j", j=PACK))
         a_sb = keep.tile([P, B * DV], BF16)
-        nc.sync.dma_start(out=a_sb[:].rearrange("t (b k) -> t b k", b=B), in_=xv_v1.rearrange("b t k -> t b k"))
         x_sb = keep.tile([P, B * C], BF16)
         for h in range(HALVES):
             nc.sync.dma_start(
                 out=x_sb[:, 2 * h * C : (2 * h + 2) * C].rearrange("t (b c) -> t b c", b=2),
                 in_=x[2 * h : 2 * h + 2].rearrange("b t c -> t b c"),
             )
+            if h == 0:
+                nc.sync.dma_start(out=a_sb[:].rearrange("t (b k) -> t b k", b=B), in_=xv_v1.rearrange("b t k -> t b k"))
         v2_sb = keep.tile([P, C], BF16)
         nc.sync.dma_start(out=v2_sb[:], in_=v2)
         w_sb = keep.tile([P, 4 * C], BF16)
@@ -65,8 +65,8 @@ def tile_full_tmix_params_pb_s_kernel(tc, x, v_first, x_v, Wv, v0, xv_v1, v2, ou
         nc.vector.tensor_copy(out=mix[:], in_=mix_bf[:])
         stay = keep.tile([P, PACK], F32)
         nc.vector.tensor_scalar(out=stay[:], in0=mix[:], scalar1=-1.0, scalar2=1.0, op0=ALU.mult, op1=ALU.add)
-        v0_rep = keep.tile([P, C // P, P], F32)
-        nc.vector.tensor_copy(out=v0_rep[:], in_=v0_col[:].unsqueeze(2).to_broadcast([P, C // P, P]))
+        v0_col = keep.tile([P, PACK], F32)
+        nc.vector.tensor_copy(out=v0_col[:], in_=v0_bf[:])
 
         aT = keep.tile([P, B * T], BF16)
         gate = keep.tile([P, B, C], F32)
@@ -148,30 +148,31 @@ def tile_full_tmix_params_pb_s_kernel(tc, x, v_first, x_v, Wv, v0, xv_v1, v2, ou
 
         def gate_of(b):
             z = banks.tile([P, C], F32, tag="bank", name="z")
-            for m in range(C // P):
+            for j in range(PACK):
                 nc.tensor.matmul(
-                    out=z[:, m * P : (m + 1) * P],
-                    lhsT=v0_rep[:, m, :],
+                    out=z[:, j:C:PACK],
+                    lhsT=v0_col[:, j : j + 1].to_broadcast([P, P]),
                     rhs=ident_f32[:],
                     is_transpose=True,
-                    start=(m == 0),
+                    start=(j == 0),
                     stop=False,
                 )
             nc.tensor.matmul(out=z[:], lhsT=aT[:, b * T : (b + 1) * T], rhs=v2_sb[:], start=False, stop=True)
             nc.scalar.activation(out=gate[:, b, :], in_=z[:], func=ACT.Sigmoid)
             nc.gpsimd.tensor_tensor(out=from_first[:, b, :], in0=vf_sb[:, b, :], in1=gate[:, b, :], op=ALU.mult)
 
-        aT_ps = banks.tile([P, B * T], BF16, tag="bank")
-        for b in range(B):
-            nc.tensor.transpose(aT_ps[:, b * T : (b + 1) * T], a_sb[:, b * DV : (b + 1) * DV], ident_bf[:])
-        nc.vector.tensor_copy(out=aT[:], in_=aT_ps[:])
-
         pieces = [(h, u) for h in range(HALVES) for u in range(2)]
         xT = {}
         for h, u in pieces:
             xT[(h, u)] = transpose_x(h, u)
+            if (h, u) == (0, 1):
+                aT_ps = banks.tile([P, B * T], BF16, tag="bank", name="aT_ps")
+                for b in range(B):
+                    nc.tensor.transpose(aT_ps[:, b * T : (b + 1) * T], a_sb[:, b * DV : (b + 1) * DV], ident_bf[:])
         for h, u in pieces:
             keep_part(h, u, xT[(h, u)])
+        add_previous(0, 0, xT[(0, 0)])
+        nc.vector.tensor_copy(out=aT[:], in_=aT_ps[:])
         gate_of(0)
         gate_of(1)
         weights(0)
@@ -179,7 +180,6 @@ def tile_full_tmix_params_pb_s_kernel(tc, x, v_first, x_v, Wv, v0, xv_v1, v2, ou
         gate_of(2)
         gate_of(3)
 
-        add_previous(0, 0, xT[(0, 0)])
         add_previous(0, 1, xT[(0, 1)])
         first_tokens(0)
         regroup(0)

@@ -70,11 +70,11 @@ def tile_full_tmix_params_pb_s_kernel(tc, x, v_first, x_v, Wv, v0, xv_v1, v2, ou
 
         aT = keep.tile([P, B * T], BF16)
         gate = keep.tile([P, B, C], F32)
-        from_first = keep.tile([P, B, C], F32)
+        first_0 = keep.tile([P, C], F32)
         x_words = x_sb[:].bitcast(F32)
         kept = keep.tile([P, HALVES, PACK, ROWS], F32)
         xv_slot = keep.tile([P, HALVES, PACK, ROWS], BF16)
-        xv_grp = keep.tile([P, HALVES, ROWS, PACK], BF16, align_bytes=64)
+        xv_grp = keep.tile([P, HALVES, ROWS, PACK], BF16, tag="reused", align_bytes=64)
         x_codes = keep.tile([P, B * T], U32, align_bytes=64)
         x_scales = keep.tile([P, B * T], U8, align_bytes=64)
         w_words = w_sb[:].bitcast(F32)
@@ -159,7 +159,9 @@ def tile_full_tmix_params_pb_s_kernel(tc, x, v_first, x_v, Wv, v0, xv_v1, v2, ou
                 )
             nc.tensor.matmul(out=z[:], lhsT=aT[:, b * T : (b + 1) * T], rhs=v2_sb[:], start=False, stop=True)
             nc.scalar.activation(out=gate[:, b, :], in_=z[:], func=ACT.Sigmoid)
-            nc.gpsimd.tensor_tensor(out=from_first[:, b, :], in0=vf_sb[:, b, :], in1=gate[:, b, :], op=ALU.mult)
+
+        def first_share(b, share):
+            nc.gpsimd.tensor_tensor(out=share, in0=vf_sb[:, b, :], in1=gate[:, b, :], op=ALU.mult)
 
         pieces = [(h, u) for h in range(HALVES) for u in range(2)]
         xT = {}
@@ -174,6 +176,7 @@ def tile_full_tmix_params_pb_s_kernel(tc, x, v_first, x_v, Wv, v0, xv_v1, v2, ou
         add_previous(0, 0, xT[(0, 0)])
         nc.vector.tensor_copy(out=aT[:], in_=aT_ps[:])
         gate_of(0)
+        first_share(0, first_0[:])
         gate_of(1)
         weights(0)
         weights(1)
@@ -191,6 +194,10 @@ def tile_full_tmix_params_pb_s_kernel(tc, x, v_first, x_v, Wv, v0, xv_v1, v2, ou
         nc.vector.quantize_mx(out=w_codes[:].bitcast(FP8X4), scales=w_scales[:], in_=w_grp[:])
         quantise_x(1)
 
+        late = keep.tile([P, B - 1, C], F32, tag="reused", align_bytes=64)
+        shares = [first_0[:]] + [late[:, b - 1, :] for b in range(1, B)]
+        for b in range(1, B):
+            first_share(b, shares[b])
         for b in range(B):
             toks = slice(b * T, (b + 1) * T)
             p_ps = banks.tile([P, C], F32, tag="bank")
@@ -206,7 +213,7 @@ def tile_full_tmix_params_pb_s_kernel(tc, x, v_first, x_v, Wv, v0, xv_v1, v2, ou
             nc.vector.scalar_tensor_tensor(
                 out=minus_p[:, b, :], in0=gate[:, b, :], scalar=1.0, in1=p_ps[:], op0=ALU.subtract, op1=ALU.mult
             )
-            engine = nc.gpsimd if b < B // 2 else nc.vector
-            engine.tensor_tensor(out=res[:, b, :], in0=from_first[:, b, :], in1=minus_p[:, b, :], op=ALU.subtract)
-            queue = nc.scalar if b < B // 2 else nc.sync
+        for b in range(B):
+            nc.vector.tensor_tensor(out=res[:, b, :], in0=shares[b], in1=minus_p[:, b, :], op=ALU.subtract)
+            queue = nc.scalar if b % 2 == 0 else nc.sync
             queue.dma_start(out=out[b], in_=res[:, b, :])

@@ -72,7 +72,8 @@ def tile_full_tmix_params_pb_s_kernel(tc, x, v_first, x_v, Wv, v0, xv_v1, v2, ou
         gate = keep.tile([P, B, C], F32)
         first_0 = keep.tile([P, C], F32)
         x_words = x_sb[:].bitcast(F32)
-        kept = keep.tile([P, HALVES, PACK, ROWS], F32)
+        moved = keep.tile([P, HALVES, PACK, ROWS], F32)
+        nc.vector.memset(moved[:].rearrange("p h j (l t) -> p (h j l) t", l=2)[:, :, 0:1], 0.0)
         xv_slot = keep.tile([P, HALVES, PACK, ROWS], BF16)
         xv_grp = keep.tile([P, HALVES, ROWS, PACK], BF16, tag="reused", align_bytes=64)
         x_codes = keep.tile([P, B * T], U32, align_bytes=64)
@@ -95,29 +96,24 @@ def tile_full_tmix_params_pb_s_kernel(tc, x, v_first, x_v, Wv, v0, xv_v1, v2, ou
                 nc.tensor.transpose(bank[:, l * T : (l + 1) * T], x_words[:, row + u : row + WORDS : 2], ident_f32[:])
             return bank[:].bitcast(BF16).rearrange("p (l t e) -> p l t e", l=2, e=2)
 
-        def keep_part(h, u, xT):
+        def move_part(h, u, xT):
             for e in range(2):
                 j = 2 * u + e
                 nc.scalar.activation(
-                    out=by_sequence(kept[:, h, j, :]), in_=xT[:, :, :, e], func=ACT.Copy, scale=stay[:, j : j + 1]
+                    out=by_sequence(moved[:, h, j, :])[:, :, 1:T],
+                    in_=xT[:, :, 0 : T - 1, e],
+                    func=ACT.Copy,
+                    scale=mix[:, j : j + 1],
                 )
 
-        def add_previous(h, u, xT):
-            for e in range(2):
-                j = 2 * u + e
-                nc.vector.scalar_tensor_tensor(
-                    out=by_sequence(xv_slot[:, h, j, :])[:, :, 1:T],
-                    in0=xT[:, :, 0 : T - 1, e],
-                    scalar=mix[:, j : j + 1],
-                    in1=by_sequence(kept[:, h, j, :])[:, :, 1:T],
-                    op0=ALU.mult,
-                    op1=ALU.add,
-                )
-
-        def first_tokens(h):
-            nc.vector.tensor_copy(
-                out=xv_slot[:, h].rearrange("p j (l t) -> p j l t", l=2)[:, :, :, 0],
-                in_=kept[:, h].rearrange("p j (l t) -> p j l t", l=2)[:, :, :, 0],
+        def add_own(h, j, xT):
+            nc.vector.scalar_tensor_tensor(
+                out=by_sequence(xv_slot[:, h, j, :]),
+                in0=xT[:, :, :, j % 2],
+                scalar=stay[:, j : j + 1],
+                in1=by_sequence(moved[:, h, j, :]),
+                op0=ALU.mult,
+                op1=ALU.add,
             )
 
         def regroup(h):
@@ -172,24 +168,26 @@ def tile_full_tmix_params_pb_s_kernel(tc, x, v_first, x_v, Wv, v0, xv_v1, v2, ou
                 for b in range(B):
                     nc.tensor.transpose(aT_ps[:, b * T : (b + 1) * T], a_sb[:, b * DV : (b + 1) * DV], ident_bf[:])
         for h, u in pieces:
-            keep_part(h, u, xT[(h, u)])
-        add_previous(0, 0, xT[(0, 0)])
+            move_part(h, u, xT[(h, u)])
+        add_own(0, 0, xT[(0, 0)])
         nc.vector.tensor_copy(out=aT[:], in_=aT_ps[:])
+        add_own(0, 1, xT[(0, 0)])
         gate_of(0)
         first_share(0, first_0[:])
-        gate_of(1)
         weights(0)
         weights(1)
+        gate_of(1)
         gate_of(2)
         gate_of(3)
 
-        add_previous(0, 1, xT[(0, 1)])
-        first_tokens(0)
+        add_own(0, 2, xT[(0, 1)])
+        add_own(0, 3, xT[(0, 1)])
+        add_own(1, 0, xT[(1, 0)])
+        add_own(1, 1, xT[(1, 0)])
         regroup(0)
-        add_previous(1, 0, xT[(1, 0)])
-        add_previous(1, 1, xT[(1, 1)])
+        add_own(1, 2, xT[(1, 1)])
+        add_own(1, 3, xT[(1, 1)])
         quantise_x(0)
-        first_tokens(1)
         regroup(1)
         nc.vector.quantize_mx(out=w_codes[:].bitcast(FP8X4), scales=w_scales[:], in_=w_grp[:])
         quantise_x(1)

@@ -34,20 +34,17 @@ def tile_full_tmix_params_pb_s_kernel(tc, x, v_first, x_v, Wv, v0, xv_v1, v2, ou
         nc.scalar.dma_start(out=v0_bf[:], in_=v0.rearrange("(p j) -> p j", j=PACK))
         a_sb = keep.tile([P, B * DV], BF16)
         x_sb = keep.tile([P, B * C], BF16)
-        for h in range(HALVES):
-            nc.sync.dma_start(
-                out=x_sb[:, 2 * h * C : (2 * h + 2) * C].rearrange("t (b c) -> t b c", b=2),
-                in_=x[2 * h : 2 * h + 2].rearrange("b t c -> t b c"),
-            )
-            if h == 0:
-                nc.sync.dma_start(out=a_sb[:].rearrange("t (b k) -> t b k", b=B), in_=xv_v1.rearrange("b t k -> t b k"))
+        for b in range(2):
+            nc.sync.dma_start(out=x_sb[:, b * C : (b + 1) * C], in_=x[b])
+        nc.sync.dma_start(out=x_sb[:, 2 * C :], in_=x[2:].rearrange("b (q i) c -> (b q) (i c)", i=2))
+        nc.sync.dma_start(out=a_sb[:].rearrange("t (b k) -> t b k", b=B), in_=xv_v1.rearrange("b t k -> t b k"))
         v2_sb = keep.tile([P, C], BF16)
         nc.sync.dma_start(out=v2_sb[:], in_=v2)
         w_sb = keep.tile([P, 4 * C], BF16)
         for h in range(HALVES):
             nc.sync.dma_start(
-                out=w_sb[:, 2 * h * C : (2 * h + 2) * C].rearrange("o (m k) -> o m k", m=2),
-                in_=Wv[h * ROWS : (h + 1) * ROWS, :].rearrange("(m o) k -> o m k", o=P),
+                out=w_sb[:, 2 * h * C : (2 * h + 2) * C],
+                in_=Wv[h * ROWS : (h + 1) * ROWS, :].rearrange("(q i) k -> q (i k)", i=2),
             )
         vf_sb = keep.tile([P, B, C], BF16)
         nc.sync.dma_start(out=vf_sb[:], in_=v_first.rearrange("b t c -> t b c"))
@@ -55,6 +52,9 @@ def tile_full_tmix_params_pb_s_kernel(tc, x, v_first, x_v, Wv, v0, xv_v1, v2, ou
         warm = keep.tile([P, 1], F32)
         nc.vector.memset(warm[:], 0.0)
         nc.scalar.activation(out=warm[:], in_=warm[:], func=ACT.Sigmoid)
+
+        moved = keep.tile([P, HALVES, PACK, ROWS], F32)
+        nc.vector.memset(moved[:].rearrange("p h j (l t) -> p (h j l) t", l=2)[:, :, 0:1], 0.0)
 
         ident_bf = keep.tile([P, P], BF16)
         make_identity(nc, ident_bf[:])
@@ -72,8 +72,6 @@ def tile_full_tmix_params_pb_s_kernel(tc, x, v_first, x_v, Wv, v0, xv_v1, v2, ou
         gate = keep.tile([P, B, C], F32)
         first_0 = keep.tile([P, C], F32)
         x_words = x_sb[:].bitcast(F32)
-        moved = keep.tile([P, HALVES, PACK, ROWS], F32)
-        nc.vector.memset(moved[:].rearrange("p h j (l t) -> p (h j l) t", l=2)[:, :, 0:1], 0.0)
         xv_slot = keep.tile([P, HALVES, PACK, ROWS], BF16)
         xv_grp = keep.tile([P, HALVES, ROWS, PACK], BF16, tag="reused", align_bytes=64)
         x_codes = keep.tile([P, B * T], U32, align_bytes=64)
@@ -89,29 +87,26 @@ def tile_full_tmix_params_pb_s_kernel(tc, x, v_first, x_v, Wv, v0, xv_v1, v2, ou
         def by_sequence(plane):
             return plane.rearrange("p (l t) -> p l t", l=2)
 
-        def transpose_x(h, u):
-            bank = banks.tile([P, ROWS], F32, tag="bank", name="x_bank")
-            for l in range(2):
-                row = (2 * h + l) * WORDS
-                nc.tensor.transpose(bank[:, l * T : (l + 1) * T], x_words[:, row + u : row + WORDS : 2], ident_f32[:])
-            return bank[:].bitcast(BF16).rearrange("p (l t e) -> p l t e", l=2, e=2)
+        def transpose_x(cols, u, width):
+            bank = banks.tile([P, width], F32, tag="bank", name="x_bank")
+            for out_cols, row in cols:
+                nc.tensor.transpose(bank[:, out_cols], x_words[:, row * WORDS + u : (row + 1) * WORDS : 2], ident_f32[:])
+            return bank[:].bitcast(BF16).rearrange("p (l t e) -> p l t e", t=T, e=2)
 
-        def move_part(h, u, xT):
-            for e in range(2):
-                j = 2 * u + e
-                nc.scalar.activation(
-                    out=by_sequence(moved[:, h, j, :])[:, :, 1:T],
-                    in_=xT[:, :, 0 : T - 1, e],
-                    func=ACT.Copy,
-                    scale=mix[:, j : j + 1],
-                )
+        def move_part(h, j, seqs, xT):
+            nc.scalar.activation(
+                out=by_sequence(moved[:, h, j, :])[:, seqs, 1:T],
+                in_=xT[:, :, 0 : T - 1, j % 2],
+                func=ACT.Copy,
+                scale=mix[:, j : j + 1],
+            )
 
-        def add_own(h, j, xT):
+        def add_own(h, j, seqs, xT):
             nc.vector.scalar_tensor_tensor(
-                out=by_sequence(xv_slot[:, h, j, :]),
+                out=by_sequence(xv_slot[:, h, j, :])[:, seqs, :],
                 in0=xT[:, :, :, j % 2],
                 scalar=stay[:, j : j + 1],
-                in1=by_sequence(moved[:, h, j, :]),
+                in1=by_sequence(moved[:, h, j, :])[:, seqs, :],
                 op0=ALU.mult,
                 op1=ALU.add,
             )
@@ -132,11 +127,12 @@ def tile_full_tmix_params_pb_s_kernel(tc, x, v_first, x_v, Wv, v0, xv_v1, v2, ou
 
         def weights(h):
             bank = banks.tile([P, 2 * ROWS], F32, tag="bank", name="w_bank")
-            view = bank[:].rearrange("p (u l o) -> p u l o", u=2, l=2)
-            for l in range(2):
+            for i in range(2):
                 for u in range(2):
-                    row = (2 * h + l) * WORDS
-                    nc.tensor.transpose(view[:, u, l, :], w_words[:, row + u : row + WORDS : 2], ident_f32[:])
+                    row = (2 * h + i) * WORDS
+                    nc.tensor.transpose(
+                        bank[:, u * ROWS + i : (u + 1) * ROWS : 2], w_words[:, row + u : row + WORDS : 2], ident_f32[:]
+                    )
             nc.scalar.copy(
                 out=w_grp_words[:, h * ROWS : (h + 1) * ROWS, :],
                 in_=bank[:].rearrange("p (u o) -> p o u", u=2),
@@ -159,34 +155,39 @@ def tile_full_tmix_params_pb_s_kernel(tc, x, v_first, x_v, Wv, v0, xv_v1, v2, ou
         def first_share(b, share):
             nc.gpsimd.tensor_tensor(out=share, in0=vf_sb[:, b, :], in1=gate[:, b, :], op=ALU.mult)
 
-        pieces = [(h, u) for h in range(HALVES) for u in range(2)]
-        xT = {}
-        for h, u in pieces:
-            xT[(h, u)] = transpose_x(h, u)
-            if (h, u) == (0, 1):
-                aT_ps = banks.tile([P, B * T], BF16, tag="bank", name="aT_ps")
-                for b in range(B):
-                    nc.tensor.transpose(aT_ps[:, b * T : (b + 1) * T], a_sb[:, b * DV : (b + 1) * DV], ident_bf[:])
-        for h, u in pieces:
-            move_part(h, u, xT[(h, u)])
-        add_own(0, 0, xT[(0, 0)])
+        first, second, both = slice(0, 1), slice(1, 2), slice(0, 2)
+        lone = slice(0, T)
+        by_rows = [(slice(0, T), 0), (slice(T, ROWS), 1)]
+        by_pairs = [(slice(0, ROWS, 2), 2), (slice(1, ROWS, 2), 3)]
+        x_first = transpose_x([(lone, 0)], 0, T)
+        x_second = transpose_x([(lone, 1)], 0, T)
+        x_01 = transpose_x(by_rows, 1, ROWS)
+        x_10 = transpose_x(by_pairs, 0, ROWS)
+        x_11 = transpose_x(by_pairs, 1, ROWS)
+        aT_ps = banks.tile([P, B * T], BF16, tag="bank", name="aT_ps")
+        for b in range(B):
+            nc.tensor.transpose(aT_ps[:, b * T : (b + 1) * T], a_sb[:, b * DV : (b + 1) * DV], ident_bf[:])
+        early = [(0, 0, first, x_first), (0, 1, first, x_first), (0, 0, second, x_second), (0, 1, second, x_second)]
+        later = [(0, 2, both, x_01), (0, 3, both, x_01), (1, 0, both, x_10), (1, 1, both, x_10)]
+        last = [(1, 2, both, x_11), (1, 3, both, x_11)]
+        for piece in early + later + last:
+            move_part(*piece)
+        for piece in early + later[:2]:
+            add_own(*piece)
         nc.vector.tensor_copy(out=aT[:], in_=aT_ps[:])
-        add_own(0, 1, xT[(0, 0)])
+        weights(0)
         gate_of(0)
         first_share(0, first_0[:])
-        weights(0)
         weights(1)
         gate_of(1)
         gate_of(2)
         gate_of(3)
 
-        add_own(0, 2, xT[(0, 1)])
-        add_own(0, 3, xT[(0, 1)])
-        add_own(1, 0, xT[(1, 0)])
-        add_own(1, 1, xT[(1, 0)])
+        for piece in later[2:]:
+            add_own(*piece)
         regroup(0)
-        add_own(1, 2, xT[(1, 1)])
-        add_own(1, 3, xT[(1, 1)])
+        for piece in last:
+            add_own(*piece)
         quantise_x(0)
         regroup(1)
         nc.vector.quantize_mx(out=w_codes[:].bitcast(FP8X4), scales=w_scales[:], in_=w_grp[:])
@@ -196,9 +197,9 @@ def tile_full_tmix_params_pb_s_kernel(tc, x, v_first, x_v, Wv, v0, xv_v1, v2, ou
         shares = [first_0[:]] + [late[:, b - 1, :] for b in range(1, B)]
         for b in range(1, B):
             first_share(b, shares[b])
-        for b in range(B):
+        def project(b):
             toks = slice(b * T, (b + 1) * T)
-            p_ps = banks.tile([P, C], F32, tag="bank")
+            p_ps = banks.tile([P, C], F32, tag="bank", name="p_ps")
             nc.tensor.matmul_mx(
                 out=p_ps[:],
                 lhsT=x_codes[:, toks].bitcast(FP8X4),
@@ -211,7 +212,18 @@ def tile_full_tmix_params_pb_s_kernel(tc, x, v_first, x_v, Wv, v0, xv_v1, v2, ou
             nc.vector.scalar_tensor_tensor(
                 out=minus_p[:, b, :], in0=gate[:, b, :], scalar=1.0, in1=p_ps[:], op0=ALU.subtract, op1=ALU.mult
             )
-        for b in range(B):
-            nc.vector.tensor_tensor(out=res[:, b, :], in0=shares[b], in1=minus_p[:, b, :], op=ALU.subtract)
-            queue = nc.scalar if b % 2 == 0 else nc.sync
-            queue.dma_start(out=out[b], in_=res[:, b, :])
+
+        def blend(b, cols, queue):
+            nc.vector.tensor_tensor(
+                out=res[:, b, cols], in0=shares[b][:, cols], in1=minus_p[:, b, cols], op=ALU.subtract
+            )
+            queue.dma_start(out=out[b, :, cols], in_=res[:, b, cols])
+
+        for b in range(B - 1):
+            project(b)
+        blend(0, slice(0, C), nc.scalar)
+        project(B - 1)
+        blend(1, slice(0, C), nc.sync)
+        blend(2, slice(0, C), nc.scalar)
+        blend(B - 1, slice(0, C // 2), nc.sync)
+        blend(B - 1, slice(C // 2, C), nc.scalar)

@@ -70,7 +70,9 @@ def tile_full_tmix_params_pb_s_kernel(tc, x, v_first, x_v, Wv, v0, xv_v1, v2, ou
 
         aT = keep.tile([P, B * T], BF16)
         gate = keep.tile([P, B, C], F32)
-        first_0 = keep.tile([P, C], F32)
+        minus_first_0 = keep.tile([P, C], F32)
+        first_1 = keep.tile([P, C], F32)
+        turned_0 = keep.tile([P, C], F32)
         x_words = x_sb[:].bitcast(F32)
         xv_slot = keep.tile([P, HALVES, PACK, ROWS], BF16)
         xv_grp = keep.tile([P, HALVES, ROWS, PACK], BF16, tag="reused", align_bytes=64)
@@ -152,8 +154,8 @@ def tile_full_tmix_params_pb_s_kernel(tc, x, v_first, x_v, Wv, v0, xv_v1, v2, ou
             nc.tensor.matmul(out=z[:], lhsT=aT[:, b * T : (b + 1) * T], rhs=v2_sb[:], start=False, stop=True)
             nc.scalar.activation(out=gate[:, b, :], in_=z[:], func=ACT.Sigmoid)
 
-        def first_share(b, share):
-            nc.gpsimd.tensor_tensor(out=share, in0=vf_sb[:, b, :], in1=gate[:, b, :], op=ALU.mult)
+        def first_share(share, first, b):
+            nc.gpsimd.tensor_tensor(out=share, in0=first, in1=gate[:, b, :], op=ALU.mult)
 
         first, second, both = slice(0, 1), slice(1, 2), slice(0, 2)
         lone = slice(0, T)
@@ -177,7 +179,6 @@ def tile_full_tmix_params_pb_s_kernel(tc, x, v_first, x_v, Wv, v0, xv_v1, v2, ou
         nc.vector.tensor_copy(out=aT[:], in_=aT_ps[:])
         weights(0)
         gate_of(0)
-        first_share(0, first_0[:])
         weights(1)
         gate_of(1)
         gate_of(2)
@@ -190,13 +191,18 @@ def tile_full_tmix_params_pb_s_kernel(tc, x, v_first, x_v, Wv, v0, xv_v1, v2, ou
             add_own(*piece)
         quantise_x(0)
         regroup(1)
+        nc.vector.scalar_tensor_tensor(
+            out=minus_first_0[:], in0=gate[:, 0, :], scalar=-1.0, in1=vf_sb[:, 0, :], op0=ALU.mult, op1=ALU.mult
+        )
         nc.vector.quantize_mx(out=w_codes[:].bitcast(FP8X4), scales=w_scales[:], in_=w_grp[:])
         quantise_x(1)
 
-        late = keep.tile([P, B - 1, C], F32, tag="reused", align_bytes=64)
-        shares = [first_0[:]] + [late[:, b - 1, :] for b in range(1, B)]
-        for b in range(1, B):
-            first_share(b, shares[b])
+        nc.vector.tensor_tensor(out=first_1[:], in0=vf_sb[:, 1, :], in1=gate[:, 1, :], op=ALU.mult)
+        late = keep.tile([P, 2, C], F32, tag="reused", align_bytes=64)
+        firsts = {1: first_1[:], 2: late[:, 0, :], 3: late[:, 1, :]}
+        for b in (2, 3):
+            first_share(firsts[b], vf_sb[:, b, :], b)
+
         def project(b):
             toks = slice(b * T, (b + 1) * T)
             p_ps = banks.tile([P, C], F32, tag="bank", name="p_ps")
@@ -215,14 +221,44 @@ def tile_full_tmix_params_pb_s_kernel(tc, x, v_first, x_v, Wv, v0, xv_v1, v2, ou
 
         def blend(b, cols, queue):
             nc.vector.tensor_tensor(
-                out=res[:, b, cols], in0=shares[b][:, cols], in1=minus_p[:, b, cols], op=ALU.subtract
+                out=res[:, b, cols], in0=firsts[b][:, cols], in1=minus_p[:, b, cols], op=ALU.subtract
             )
             queue.dma_start(out=out[b, :, cols], in_=res[:, b, cols])
 
-        for b in range(B - 1):
-            project(b)
-        blend(0, slice(0, C), nc.scalar)
-        project(B - 1)
+        project(0)
+        project(1)
+        blocks = [slice(m * P, (m + 1) * P) for m in range(C // P)]
+        halves = [blocks[:2], blocks[2:]]
+        sums = [banks.tile([P, C // 2], F32, tag="bank", name="sum_a"), banks.tile([P, C // 2], F32, tag="bank", name="sum_b")]
+
+        def add_transposed(addend, opens):
+            for half, total in zip(halves, sums):
+                for i, block in enumerate(half):
+                    nc.tensor.matmul(
+                        out=total[:, blocks[i]],
+                        lhsT=addend[:, block],
+                        rhs=ident_f32[:],
+                        is_transpose=True,
+                        start=(opens and i == 0),
+                        stop=(not opens and i == 1),
+                    )
+
+        add_transposed(minus_first_0[:], opens=True)
+        project(2)
+        project(3)
+        add_transposed(minus_p[:, 0, :], opens=False)
+        backs = []
+        for half, total in zip(halves, sums):
+            cols = slice(half[0].start, half[1].stop)
+            nc.scalar.copy(out=turned_0[:, cols], in_=total[:])
+            back = banks.tile([P, C // 2], F32, tag="bank", name="back")
+            for i, block in enumerate(half):
+                nc.tensor.transpose(back[:, blocks[i]], turned_0[:, block], ident_f32[:])
+            backs.append((cols, back))
+        for cols, back in backs:
+            nc.scalar.activation(out=res[:, 0, cols], in_=back[:], func=ACT.Copy, scale=-1.0)
+        nc.scalar.dma_start(out=out[0], in_=res[:, 0, :])
+
         blend(1, slice(0, C), nc.sync)
         blend(2, slice(0, C), nc.scalar)
         blend(B - 1, slice(0, C // 2), nc.sync)

@@ -71,7 +71,6 @@ def tile_full_tmix_params_pb_s_kernel(tc, x, v_first, x_v, Wv, v0, xv_v1, v2, ou
         aT = keep.tile([P, B * T], BF16)
         gate = keep.tile([P, B, C], F32)
         minus_first_0 = keep.tile([P, C], F32)
-        first_1 = keep.tile([P, C], F32)
         turned_0 = keep.tile([P, C], F32)
         x_words = x_sb[:].bitcast(F32)
         xv_slot = keep.tile([P, HALVES, PACK, ROWS], BF16)
@@ -113,18 +112,19 @@ def tile_full_tmix_params_pb_s_kernel(tc, x, v_first, x_v, Wv, v0, xv_v1, v2, ou
                 op1=ALU.add,
             )
 
-        def regroup(h):
-            nc.vector.tensor_copy(
-                out=xv_grp[:, h].rearrange("p (c i) j -> p c j i", i=4),
-                in_=xv_slot[:, h].rearrange("p j (c i) -> p c j i", i=4),
+        def regroup(row, width, copy):
+            h, first = divmod(row, ROWS)
+            copy(
+                out=xv_grp[:, h, first : first + width].rearrange("p (c i) j -> p c j i", i=4),
+                in_=xv_slot[:, h, :, first : first + width].rearrange("p j (c i) -> p c j i", i=4),
             )
 
-        def quantise_x(h):
-            cols = slice(h * ROWS, (h + 1) * ROWS)
+        def quantise_x(row, width):
+            h, first = divmod(row, ROWS)
             nc.vector.quantize_mx(
-                out=x_codes[:, cols].bitcast(FP8X4),
-                scales=x_scales[:, cols],
-                in_=xv_grp[:, h].rearrange("p r j -> p (r j)"),
+                out=x_codes[:, row : row + width].bitcast(FP8X4),
+                scales=x_scales[:, row : row + width],
+                in_=xv_grp[:, h, first : first + width].rearrange("p r j -> p (r j)"),
             )
 
         def weights(h):
@@ -180,28 +180,27 @@ def tile_full_tmix_params_pb_s_kernel(tc, x, v_first, x_v, Wv, v0, xv_v1, v2, ou
         weights(0)
         gate_of(0)
         weights(1)
-        gate_of(1)
-        gate_of(2)
-        gate_of(3)
 
         for piece in later[2:]:
             add_own(*piece)
-        regroup(0)
+        regroup(0, ROWS, nc.vector.tensor_copy)
         for piece in last:
             add_own(*piece)
-        quantise_x(0)
-        regroup(1)
+        regroup(ROWS + T, T, nc.scalar.copy)
+        for b in range(1, B):
+            gate_of(b)
+        quantise_x(0, ROWS)
+        regroup(ROWS, T, nc.vector.tensor_copy)
         nc.vector.scalar_tensor_tensor(
             out=minus_first_0[:], in0=gate[:, 0, :], scalar=-1.0, in1=vf_sb[:, 0, :], op0=ALU.mult, op1=ALU.mult
         )
         nc.vector.quantize_mx(out=w_codes[:].bitcast(FP8X4), scales=w_scales[:], in_=w_grp[:])
-        quantise_x(1)
+        quantise_x(ROWS, ROWS)
 
+        first_1 = keep.tile([P, C], F32, tag="shared")
         nc.vector.tensor_tensor(out=first_1[:], in0=vf_sb[:, 1, :], in1=gate[:, 1, :], op=ALU.mult)
-        late = keep.tile([P, 2, C], F32, tag="reused", align_bytes=64)
-        firsts = {1: first_1[:], 2: late[:, 0, :], 3: late[:, 1, :]}
-        for b in (2, 3):
-            first_share(firsts[b], vf_sb[:, b, :], b)
+        first_2 = keep.tile([P, C], F32, tag="reused", align_bytes=64)
+        first_share(first_2[:], vf_sb[:, 2, :], 2)
 
         def project(b):
             toks = slice(b * T, (b + 1) * T)
@@ -219,10 +218,8 @@ def tile_full_tmix_params_pb_s_kernel(tc, x, v_first, x_v, Wv, v0, xv_v1, v2, ou
                 out=minus_p[:, b, :], in0=gate[:, b, :], scalar=1.0, in1=p_ps[:], op0=ALU.subtract, op1=ALU.mult
             )
 
-        def blend(b, cols, queue):
-            nc.vector.tensor_tensor(
-                out=res[:, b, cols], in0=firsts[b][:, cols], in1=minus_p[:, b, cols], op=ALU.subtract
-            )
+        def blend(b, first, cols, queue):
+            nc.vector.tensor_tensor(out=res[:, b, cols], in0=first[:, cols], in1=minus_p[:, b, cols], op=ALU.subtract)
             queue.dma_start(out=out[b, :, cols], in_=res[:, b, cols])
 
         project(0)
@@ -244,6 +241,9 @@ def tile_full_tmix_params_pb_s_kernel(tc, x, v_first, x_v, Wv, v0, xv_v1, v2, ou
                     )
 
         add_transposed(minus_first_0[:], opens=True)
+        blend(1, first_1, slice(0, C), nc.sync)
+        first_3 = keep.tile([P, C], F32, tag="shared")
+        first_share(first_3[:], vf_sb[:, 3, :], 3)
         project(2)
         project(3)
         add_transposed(minus_p[:, 0, :], opens=False)
@@ -259,7 +259,6 @@ def tile_full_tmix_params_pb_s_kernel(tc, x, v_first, x_v, Wv, v0, xv_v1, v2, ou
             nc.scalar.activation(out=res[:, 0, cols], in_=back[:], func=ACT.Copy, scale=-1.0)
         nc.scalar.dma_start(out=out[0], in_=res[:, 0, :])
 
-        blend(1, slice(0, C), nc.sync)
-        blend(2, slice(0, C), nc.scalar)
-        blend(B - 1, slice(0, C // 2), nc.sync)
-        blend(B - 1, slice(C // 2, C), nc.scalar)
+        blend(2, first_2, slice(0, C), nc.sync)
+        blend(3, first_3, slice(0, C // 2), nc.scalar)
+        blend(3, first_3, slice(C // 2, C), nc.sync)

from contextlib import ExitStack

import concourse.mybir as mybir
from concourse.masks import make_identity

BF16 = mybir.dt.bfloat16
F32 = mybir.dt.float32
U32 = mybir.dt.uint32
U8 = mybir.dt.uint8
FP8X4 = mybir.dt.float8_e4m3fn_x4
ALU = mybir.AluOpType
ACT = mybir.ActivationFunctionType

P = 128
B, T, C, DV = 4, 128, 512, 128
PACK = 4
HALVES = 2
ROWS = 256
WORDS = C // 2

FLOPS = 2 * B * T * C * C + 2 * B * T * DV * C


def tile_full_tmix_params_pb_s_kernel(tc, x, v_first, x_v, Wv, v0, xv_v1, v2, out):
    nc = tc.nc
    with ExitStack() as ctx:
        keep = ctx.enter_context(tc.tile_pool(name="keep", bufs=1))
        banks = ctx.enter_context(tc.psum_pool(name="banks", bufs=8))
        ctx.enter_context(tc.manual_schedule())

        mix_bf = keep.tile([P, PACK], BF16)
        nc.scalar.dma_start(out=mix_bf[:], in_=x_v.rearrange("(p j) -> p j", j=PACK))
        v0_bf = keep.tile([P, PACK], BF16)
        nc.scalar.dma_start(out=v0_bf[:], in_=v0.rearrange("(p j) -> p j", j=PACK))
        a_sb = keep.tile([P, B * DV], BF16)
        x_sb = keep.tile([P, B * C], BF16)
        for b in range(2):
            nc.sync.dma_start(out=x_sb[:, b * C : (b + 1) * C], in_=x[b])
        nc.sync.dma_start(out=x_sb[:, 2 * C :], in_=x[2:].rearrange("b (q i) c -> (b q) (i c)", i=2))
        nc.sync.dma_start(out=a_sb[:].rearrange("t (b k) -> t b k", b=B), in_=xv_v1.rearrange("b t k -> t b k"))
        v2_sb = keep.tile([P, C], BF16)
        nc.sync.dma_start(out=v2_sb[:], in_=v2)
        w_sb = keep.tile([P, 4 * C], BF16)
        for h in range(HALVES):
            nc.sync.dma_start(
                out=w_sb[:, 2 * h * C : (2 * h + 2) * C],
                in_=Wv[h * ROWS : (h + 1) * ROWS, :].rearrange("(q i) k -> q (i k)", i=2),
            )
        vf_sb = keep.tile([P, B, C], BF16)
        nc.sync.dma_start(out=vf_sb[:], in_=v_first.rearrange("b t c -> t b c"))

        warm = keep.tile([P, 1], F32)
        nc.vector.memset(warm[:], 0.0)
        nc.scalar.activation(out=warm[:], in_=warm[:], func=ACT.Sigmoid)

        moved = keep.tile([P, HALVES, PACK, ROWS], F32)
        nc.vector.memset(moved[:].rearrange("p h j (l t) -> p (h j l) t", l=2)[:, :, 0:1], 0.0)

        ident_bf = keep.tile([P, P], BF16)
        make_identity(nc, ident_bf[:])
        ident_f32 = keep.tile([P, P], F32)
        make_identity(nc, ident_f32[:])

        mix = keep.tile([P, PACK], F32)
        nc.vector.tensor_copy(out=mix[:], in_=mix_bf[:])
        stay = keep.tile([P, PACK], F32)
        nc.vector.tensor_scalar(out=stay[:], in0=mix[:], scalar1=-1.0, scalar2=1.0, op0=ALU.mult, op1=ALU.add)
        v0_col = keep.tile([P, PACK], F32)
        nc.vector.tensor_copy(out=v0_col[:], in_=v0_bf[:])

        aT = keep.tile([P, B * T], BF16)
        gate = keep.tile([P, B, C], F32)
        minus_first_0 = keep.tile([P, C], F32)
        turned_0 = keep.tile([P, C], F32)
        x_words = x_sb[:].bitcast(F32)
        xv_slot = keep.tile([P, HALVES, PACK, ROWS], BF16)
        xv_grp = keep.tile([P, HALVES, ROWS, PACK], BF16, tag="reused", align_bytes=64)
        x_codes = keep.tile([P, B * T], U32, align_bytes=64)
        x_scales = keep.tile([P, B * T], U8, align_bytes=64)
        w_words = w_sb[:].bitcast(F32)
        w_grp = keep.tile([P, C * PACK], BF16, align_bytes=64)
        w_grp_words = w_grp[:].bitcast(F32).rearrange("p (o u) -> p o u", u=2)
        w_codes = keep.tile([P, C], U32, align_bytes=64)
        w_scales = keep.tile([P, C], U8, align_bytes=64)
        minus_p = keep.tile([P, B, C], F32)
        res = keep.tile([P, B, C], F32)

        def by_sequence(plane):
            return plane.rearrange("p (l t) -> p l t", l=2)

        def transpose_x(cols, u, width):
            bank = banks.tile([P, width], F32, tag="bank", name="x_bank")
            for out_cols, row in cols:
                nc.tensor.transpose(bank[:, out_cols], x_words[:, row * WORDS + u : (row + 1) * WORDS : 2], ident_f32[:])
            return bank[:].bitcast(BF16).rearrange("p (l t e) -> p l t e", t=T, e=2)

        def move_part(h, j, seqs, xT):
            nc.scalar.activation(
                out=by_sequence(moved[:, h, j, :])[:, seqs, 1:T],
                in_=xT[:, :, 0 : T - 1, j % 2],
                func=ACT.Copy,
                scale=mix[:, j : j + 1],
            )

        def add_own(h, j, seqs, xT):
            nc.vector.scalar_tensor_tensor(
                out=by_sequence(xv_slot[:, h, j, :])[:, seqs, :],
                in0=xT[:, :, :, j % 2],
                scalar=stay[:, j : j + 1],
                in1=by_sequence(moved[:, h, j, :])[:, seqs, :],
                op0=ALU.mult,
                op1=ALU.add,
            )

        def regroup(row, width, copy):
            h, first = divmod(row, ROWS)
            copy(
                out=xv_grp[:, h, first : first + width].rearrange("p (c i) j -> p c j i", i=4),
                in_=xv_slot[:, h, :, first : first + width].rearrange("p j (c i) -> p c j i", i=4),
            )

        def quantise_x(row, width):
            h, first = divmod(row, ROWS)
            nc.vector.quantize_mx(
                out=x_codes[:, row : row + width].bitcast(FP8X4),
                scales=x_scales[:, row : row + width],
                in_=xv_grp[:, h, first : first + width].rearrange("p r j -> p (r j)"),
            )

        def weights(h):
            bank = banks.tile([P, 2 * ROWS], F32, tag="bank", name="w_bank")
            for i in range(2):
                for u in range(2):
                    row = (2 * h + i) * WORDS
                    nc.tensor.transpose(
                        bank[:, u * ROWS + i : (u + 1) * ROWS : 2], w_words[:, row + u : row + WORDS : 2], ident_f32[:]
                    )
            nc.scalar.copy(
                out=w_grp_words[:, h * ROWS : (h + 1) * ROWS, :],
                in_=bank[:].rearrange("p (u o) -> p o u", u=2),
            )

        def gate_of(b):
            z = banks.tile([P, C], F32, tag="bank", name="z")
            for j in range(PACK):
                nc.tensor.matmul(
                    out=z[:, j:C:PACK],
                    lhsT=v0_col[:, j : j + 1].to_broadcast([P, P]),
                    rhs=ident_f32[:],
                    is_transpose=True,
                    start=(j == 0),
                    stop=False,
                )
            nc.tensor.matmul(out=z[:], lhsT=aT[:, b * T : (b + 1) * T], rhs=v2_sb[:], start=False, stop=True)
            nc.scalar.activation(out=gate[:, b, :], in_=z[:], func=ACT.Sigmoid)

        def first_share(share, first, b):
            nc.gpsimd.tensor_tensor(out=share, in0=first, in1=gate[:, b, :], op=ALU.mult)

        first, second, both = slice(0, 1), slice(1, 2), slice(0, 2)
        lone = slice(0, T)
        by_rows = [(slice(0, T), 0), (slice(T, ROWS), 1)]
        by_pairs = [(slice(0, ROWS, 2), 2), (slice(1, ROWS, 2), 3)]
        x_first = transpose_x([(lone, 0)], 0, T)
        x_second = transpose_x([(lone, 1)], 0, T)
        x_01 = transpose_x(by_rows, 1, ROWS)
        x_10 = transpose_x(by_pairs, 0, ROWS)
        x_11 = transpose_x(by_pairs, 1, ROWS)
        aT_ps = banks.tile([P, B * T], BF16, tag="bank", name="aT_ps")
        for b in range(B):
            nc.tensor.transpose(aT_ps[:, b * T : (b + 1) * T], a_sb[:, b * DV : (b + 1) * DV], ident_bf[:])
        early = [(0, 0, first, x_first), (0, 1, first, x_first), (0, 0, second, x_second), (0, 1, second, x_second)]
        later = [(0, 2, both, x_01), (0, 3, both, x_01), (1, 0, both, x_10), (1, 1, both, x_10)]
        last = [(1, 2, both, x_11), (1, 3, both, x_11)]
        for piece in early + later + last:
            move_part(*piece)
        for piece in early + later[:2]:
            add_own(*piece)
        nc.vector.tensor_copy(out=aT[:], in_=aT_ps[:])
        weights(0)
        gate_of(0)
        weights(1)

        for piece in later[2:]:
            add_own(*piece)
        regroup(0, ROWS, nc.vector.tensor_copy)
        for piece in last:
            add_own(*piece)
        regroup(ROWS + T, T, nc.scalar.copy)
        for b in range(1, B):
            gate_of(b)
        quantise_x(0, ROWS)
        regroup(ROWS, T, nc.vector.tensor_copy)
        nc.vector.scalar_tensor_tensor(
            out=minus_first_0[:], in0=gate[:, 0, :], scalar=-1.0, in1=vf_sb[:, 0, :], op0=ALU.mult, op1=ALU.mult
        )
        nc.vector.quantize_mx(out=w_codes[:].bitcast(FP8X4), scales=w_scales[:], in_=w_grp[:])
        quantise_x(ROWS, ROWS)

        first_1 = keep.tile([P, C], F32, tag="shared")
        nc.vector.tensor_tensor(out=first_1[:], in0=vf_sb[:, 1, :], in1=gate[:, 1, :], op=ALU.mult)
        first_2 = keep.tile([P, C], F32, tag="reused", align_bytes=64)
        first_share(first_2[:], vf_sb[:, 2, :], 2)

        def project(b):
            toks = slice(b * T, (b + 1) * T)
            p_ps = banks.tile([P, C], F32, tag="bank", name="p_ps")
            nc.tensor.matmul_mx(
                out=p_ps[:],
                lhsT=x_codes[:, toks].bitcast(FP8X4),
                lhsT_scale=x_scales[:, toks],
                rhs=w_codes[:].bitcast(FP8X4),
                rhs_scale=w_scales[:],
                start=True,
                stop=True,
            )
            nc.vector.scalar_tensor_tensor(
                out=minus_p[:, b, :], in0=gate[:, b, :], scalar=1.0, in1=p_ps[:], op0=ALU.subtract, op1=ALU.mult
            )

        def blend(b, first, cols, queue):
            nc.vector.tensor_tensor(out=res[:, b, cols], in0=first[:, cols], in1=minus_p[:, b, cols], op=ALU.subtract)
            queue.dma_start(out=out[b, :, cols], in_=res[:, b, cols])

        project(0)
        project(1)
        blocks = [slice(m * P, (m + 1) * P) for m in range(C // P)]
        halves = [blocks[:2], blocks[2:]]
        sums = [banks.tile([P, C // 2], F32, tag="bank", name="sum_a"), banks.tile([P, C // 2], F32, tag="bank", name="sum_b")]

        def add_transposed(addend, opens):
            for half, total in zip(halves, sums):
                for i, block in enumerate(half):
                    nc.tensor.matmul(
                        out=total[:, blocks[i]],
                        lhsT=addend[:, block],
                        rhs=ident_f32[:],
                        is_transpose=True,
                        start=(opens and i == 0),
                        stop=(not opens and i == 1),
                    )

        add_transposed(minus_first_0[:], opens=True)
        blend(1, first_1, slice(0, C), nc.sync)
        first_3 = keep.tile([P, C], F32, tag="shared")
        first_share(first_3[:], vf_sb[:, 3, :], 3)
        project(2)
        project(3)
        add_transposed(minus_p[:, 0, :], opens=False)
        backs = []
        for half, total in zip(halves, sums):
            cols = slice(half[0].start, half[1].stop)
            nc.scalar.copy(out=turned_0[:, cols], in_=total[:])
            back = banks.tile([P, C // 2], F32, tag="bank", name="back")
            for i, block in enumerate(half):
                nc.tensor.transpose(back[:, blocks[i]], turned_0[:, block], ident_f32[:])
            backs.append((cols, back))
        for cols, back in backs:
            nc.scalar.activation(out=res[:, 0, cols], in_=back[:], func=ACT.Copy, scale=-1.0)
        nc.scalar.dma_start(out=out[0], in_=res[:, 0, :])

        blend(2, first_2, slice(0, C), nc.sync)
        blend(3, first_3, slice(0, C // 2), nc.scalar)
        blend(3, first_3, slice(C // 2, C), nc.sync)
